import numpy as np
import ml_dtypes


def mxq(x, axis, fmt="e4m3"):
    dtype, down = {"e4m3": (ml_dtypes.float8_e4m3fn, 7), "e5m2": (ml_dtypes.float8_e5m2, 14)}[fmt]
    v = np.moveaxis(np.asarray(x, np.float32).astype(ml_dtypes.bfloat16).astype(np.float64), axis, -1)
    blocks = v.reshape(v.shape[:-1] + (-1, 32))
    amax = np.abs(blocks).max(-1, keepdims=True)
    byte = np.maximum(np.where(amax > 0, np.frexp(amax)[1] - 1 + 127, 0) - down, 1)
    scale = np.exp2(byte - 127.0)
    codes = (blocks / scale).astype(np.float32).astype(dtype).astype(np.float64)
    return np.moveaxis((codes * scale).reshape(v.shape), -1, axis)


WIDE = False


def mx_kscale(k):
    if not WIDE:
        return np.ones(k)
    levels = np.array([10, -10, 5, -5, 0])
    if k % 512:
        return np.exp2(np.random.permutation(np.resize(levels, k // 32))).repeat(32)
    a = np.empty((k // 512, 16))
    for p in range(k // 512):
        a[p, :8] = np.random.permutation(np.resize(levels, 8))
        for g in range(8):
            far = levels[np.abs(levels - a[p, g]) >= 10]
            a[p, g + 8] = far[np.random.randint(len(far))]
    return np.exp2(a.ravel()).repeat(32)


BF16 = ml_dtypes.bfloat16


def bf(x):
    return np.asarray(x, np.float32).astype(BF16)


def f64(x):
    return np.asarray(x).astype(np.float64)


BS, CIN, H, D, L, P, OUT_DIM = 8, 512, 256, 1024, 10, 2, 128
K0, K1 = CIN * P, H * P


def patch_conv_relu(y, w):
    bs, cin, d = y.shape
    out, p = w.shape[0], w.shape[-1]
    q = d // p
    rows = y.reshape(bs, cin, q, p).transpose(0, 2, 1, 3).reshape(bs * q, cin * p)
    wm = w.reshape(out, cin * p).T
    z = (mxq(rows, 1, "e4m3") @ mxq(wm, 0, "e4m3")) * (1.0 / np.sqrt(cin))
    return np.maximum(z, 0.0).reshape(bs, q, out).transpose(0, 2, 1)


def draw0():
    s = mx_kscale(K0).reshape(CIN, P)
    t = mx_kscale(K1)[::P]
    return {"x": bf(np.random.standard_normal((BS, CIN, D)) * np.tile(s, (1, D // P))),
            "w0": bf(np.random.standard_normal((H, CIN, P)) / s * t[:, None, None]),
            "w1": bf(np.random.standard_normal((H, H, P)) / t[:, None])}


def core(x, w0, w1):
    h = patch_conv_relu(f64(x), f64(w0))
    return patch_conv_relu(h, f64(w1))


def e4m3fn_bytes(y):
    return np.clip(np.asarray(y, np.float64), -448.0, 448.0).astype(np.float32).astype(ml_dtypes.float8_e4m3fn).view(np.uint8)


def e4m3fn_values(b):
    return np.asarray(b, np.uint8).view(ml_dtypes.float8_e4m3fn).astype(np.float64)


def setup_inputs():
    d = draw0()
    x0 = np.asarray(d['x']).astype(np.float64)
    s = (np.max(np.abs(x0), axis=(0, 2), keepdims=True) / 448.0).astype(np.float32)
    out = {}
    for k, v in d.items():
        if k == 'x':
            out['x_bytes'] = e4m3fn_bytes(x0 / s.astype(np.float64))
            out['x_scale'] = s
        else:
            out[k] = v
    return out


def reference(x_bytes, x_scale, w0, w1):
    return core(e4m3fn_values(x_bytes) * x_scale.astype(np.float64), w0, w1)

@@ -1,0 +1,263 @@
+import math
+from contextlib import ExitStack
+
+import concourse.mybir as mybir
+from concourse.masks import make_identity
+
+BS, CIN, HID, D, OUT_DIM = 8, 512, 256, 1024, 256
+P = 128
+Q = D // 2
+R = Q // 2
+G = 2
+HALF = Q // 2
+
+FLOPS = 2 * BS * Q * HID * (2 * CIN) + 2 * BS * R * OUT_DIM * (2 * HID)
+
+F32 = mybir.dt.float32
+BF16 = mybir.dt.bfloat16
+U32 = mybir.dt.uint32
+U8 = mybir.dt.uint8
+FP8 = mybir.dt.float8_e4m3fn
+FP8X4 = mybir.dt.float8_e4m3fn_x4
+ACT = mybir.ActivationFunctionType
+ALU = mybir.AluOpType
+
+SCALE0 = 1.0 / math.sqrt(CIN)
+SCALE1 = 1.0 / math.sqrt(HID)
+
+
+def tile_cnn_pa_t_kernel(tc, x_bytes, x_scale, w0, w1, out):
+    nc = tc.nc
+
+    with ExitStack() as ctx:
+        keep = ctx.enter_context(tc.tile_pool(name="keep", bufs=1))
+        xin = ctx.enter_context(tc.tile_pool(name="xin", bufs=8))
+        work = ctx.enter_context(tc.tile_pool(name="work", bufs=3))
+        psum = ctx.enter_context(tc.psum_pool(name="psum", bufs=4))
+        ctx.enter_context(tc.manual_schedule())
+
+        sc = keep.tile([P, G, 2], F32, name="sc")
+        nc.scalar.dma_start(out=sc[:], in_=x_scale.rearrange("o (g p c) x -> p (o g) (c x)", g=G, p=P, c=2))
+        xv = x_bytes.rearrange("b (g p c) d -> b p g (c d)", g=G, p=P, c=2)
+        x_sb = []
+        for b in range(BS):
+            x_t = xin.tile([P, G, 2 * D], U8, name="x_t", align_bytes=64)
+            x_sb.append(x_t)
+        w0_sb = keep.tile([P, 2 * 2 * CIN], BF16, name="w0_sb", align_bytes=64)
+        w1_sb = keep.tile([P, 2 * 2 * HID], BF16, name="w1_sb", align_bytes=64)
+        for g, c in ((1, 0), (0, 0), (1, 1), (0, 1)):
+            nc.sync.dma_start(out=x_sb[0][:, g, c * D : (c + 1) * D], in_=xv[0][:, g, c * D : (c + 1) * D])
+        nc.sync.dma_start(out=x_sb[1][:, 1, :], in_=xv[1][:, 1, :])
+        nc.sync.dma_start(out=w0_sb[:], in_=w0.rearrange("(m t) c k -> m (t c k)", t=2))
+        nc.sync.dma_start(out=x_sb[1][:, 0, :], in_=xv[1][:, 0, :])
+        nc.sync.dma_start(out=w1_sb[:], in_=w1.rearrange("(m t) c k -> m (t c k)", t=2))
+        for b in range(2, BS):
+            nc.sync.dma_start(out=x_sb[b][:], in_=xv[b])
+
+        warm = keep.tile([P, 1], F32, name="warm")
+        nc.vector.memset(warm[:], 0.0)
+        nc.scalar.activation(out=warm[:], in_=warm[:], func=ACT.Relu)
+        ident = keep.tile([P, P], F32, name="ident")
+        make_identity(nc, ident[:])
+
+        w0_c = keep.tile([P, G * HID], U32, name="w0_c", align_bytes=64)
+        w0_s = keep.tile([P, G * HID], U8, name="w0_s", align_bytes=64)
+        w0_g = keep.tile([P, G * HID * 4], BF16, name="w0_g", align_bytes=64)
+        w1_c = keep.tile([P, OUT_DIM], U32, name="w1_c", align_bytes=64)
+        w1_s = keep.tile([P, OUT_DIM], U8, name="w1_s", align_bytes=64)
+        w1_g = keep.tile([P, OUT_DIM * 4], BF16, name="w1_g", align_bytes=64)
+
+        state = {}
+
+        def new(key, pool, shape, dtype, name):
+            if key not in state:
+                state[key] = pool.tile(shape, dtype, name=name, align_bytes=64)
+            return state[key]
+
+        def transpose_weights(w_sb, row, first, key):
+            words = w_sb[:].bitcast(F32)
+            bank = psum.tile([P, 2, 2, P], F32, name="bank2", tag="bank2")
+            for t in range(2):
+                for u in range(2):
+                    lo = row * t + first
+                    nc.tensor.transpose(bank[:, t, u, :], words[:, lo + u : lo + 256 : 2], ident[:])
+            state[key] = bank
+
+        def weights_out(engine_copy, key, dst):
+            engine_copy(
+                out=dst.bitcast(F32).rearrange("p (t m u) -> p t m u", t=2, u=2),
+                in_=state[key][:].rearrange("p t u m -> p t m u"),
+            )
+
+        def x_values(b, g, c, lo=0, n=Q):
+            return x_sb[b][:, g, c * D + 2 * lo : c * D + 2 * (lo + n)].bitcast(FP8)
+
+        def widen_v(b, g, c):
+            grp = new(("grp", b, g), work, [P, Q * 4], BF16, "grp%d" % g)
+            nc.vector.tensor_scalar(
+                out=grp[:].rearrange("p (q c k) -> p q c k", c=2, k=2)[:, :, c, :],
+                in0=x_values(b, g, c).rearrange("p (q k) -> p q k", k=2),
+                scalar1=sc[:, g, c : c + 1],
+                scalar2=None,
+                op0=ALU.mult,
+            )
+
+        def widen_s(b, g, c, lo=0, n=Q):
+            tmp = new(("tmp", b, g), work, [P, 2, D], BF16, "tmp%d" % g)
+            nc.scalar.activation(
+                out=tmp[:, c, 2 * lo : 2 * (lo + n)],
+                in_=x_values(b, g, c, lo, n),
+                func=ACT.Copy,
+                scale=sc[:, g, c : c + 1],
+            )
+
+        def interleave(b, g, lo=0, n=Q):
+            grp = new(("grp", b, g), work, [P, Q * 4], BF16, "grp%d" % g)
+            words = state["tmp", b, g][:].rearrange("p c d -> p (c d)").bitcast(F32)
+            nc.vector.tensor_copy(
+                out=grp[:, 4 * lo : 4 * (lo + n)].bitcast(F32).rearrange("p (q c) -> p q c", c=2),
+                in_=words.rearrange("p (c q) -> p q c", c=2)[:, lo : lo + n, :],
+            )
+
+        def quantize_x(b, g, lo=0, n=Q):
+            codes = new(("xc", b, g), work, [P, Q], U32, "xc%d" % g)
+            scales = new(("xs", b, g), work, [P, Q], U8, "xs%d" % g)
+            nc.vector.quantize_mx(
+                out=codes[:, lo : lo + n].bitcast(FP8X4),
+                scales=scales[:, lo : lo + n],
+                in_=state["grp", b, g][:, 4 * lo : 4 * (lo + n)],
+            )
+
+        def layer1(b, lo, n=HALF):
+            bank = psum.tile([P, 2, n], F32, name="bank1", tag="bank1")
+            cols = slice(lo, lo + n)
+            for t in range(2):
+                for g in range(G):
+                    wcols = slice(g * HID + t * P, g * HID + (t + 1) * P)
+                    nc.tensor.matmul_mx(
+                        out=bank[:, t, :],
+                        lhsT=w0_c[:, wcols].bitcast(FP8X4),
+                        lhsT_scale=w0_s[:, wcols],
+                        rhs=state["xc", b, g][:, cols].bitcast(FP8X4),
+                        rhs_scale=state["xs", b, g][:, cols],
+                        start=(g == 0),
+                        stop=(g == G - 1),
+                    )
+            state["bank1", b, lo] = bank
+
+        def hidden(engine, b, lo, n=HALF):
+            h = new(("h", b), work, [P, R * 4], BF16, "hgrp")
+            dst = h[:, 2 * lo : 2 * (lo + n)].rearrange("p (r c k) -> p r c k", c=2, k=2)
+            z = state["bank1", b, lo][:].rearrange("p c (r k) -> p r c k", k=2)
+            if engine == "S":
+                nc.scalar.activation(out=dst, in_=z, func=ACT.Relu, scale=SCALE0)
+            else:
+                nc.vector.tensor_scalar(out=dst, in0=z, scalar1=SCALE0, scalar2=0.0, op0=ALU.mult, op1=ALU.max)
+
+        def quantize_h(b, lo=0, n=R):
+            codes = new(("hc", b), work, [P, R], U32, "hc")
+            scales = new(("hs", b), work, [P, R], U8, "hs")
+            nc.vector.quantize_mx(
+                out=codes[:, lo : lo + n].bitcast(FP8X4),
+                scales=scales[:, lo : lo + n],
+                in_=state["h", b][:, 4 * lo : 4 * (lo + n)],
+            )
+
+        def layer2(b, lo=0, n=R):
+            bank = psum.tile([P, 2, n], F32, name="bank2", tag="bank2")
+            for t in range(2):
+                wcols = slice(t * P, (t + 1) * P)
+                nc.tensor.matmul_mx(
+                    out=bank[:, t, :],
+                    lhsT=w1_c[:, wcols].bitcast(FP8X4),
+                    lhsT_scale=w1_s[:, wcols],
+                    rhs=state["hc", b][:, lo : lo + n].bitcast(FP8X4),
+                    rhs_scale=state["hs", b][:, lo : lo + n],
+                    start=True,
+                    stop=True,
+                )
+            state["bank2", b, lo] = bank
+
+        def finish(engine, b, lo=0, n=R):
+            o_sb = work.tile([P, 2, n], F32, name="o_sb", tag="o_sb")
+            bank = state["bank2", b, lo]
+            if engine == "S":
+                nc.scalar.activation(out=o_sb[:], in_=bank[:], func=ACT.Relu, scale=SCALE1)
+            else:
+                nc.vector.tensor_scalar(out=o_sb[:], in0=bank[:], scalar1=SCALE1, scalar2=0.0, op0=ALU.mult, op1=ALU.max)
+            nc.sync.dma_start(out=out[b].rearrange("(m t) r -> m t r", t=2)[:, :, lo : lo + n], in_=o_sb[:])
+
+        def quantize_w(src, codes, scales):
+            nc.vector.quantize_mx(out=codes[:].bitcast(FP8X4), scales=scales[:], in_=src[:])
+
+        LAST = BS - 1
+        for c in range(2):
+            widen_s(0, 1, c)
+            widen_v(0, 0, c)
+        quantize_x(0, 0)
+        for c in range(2):
+            widen_s(1, 1, c)
+        interleave(0, 1)
+        transpose_weights(w0_sb, 512, 0, 0)
+        transpose_weights(w0_sb, 512, 256, 1)
+        transpose_weights(w1_sb, 256, 0, 2)
+        weights_out(nc.scalar.copy, 0, w0_g[:, 0 : HID * 4])
+        weights_out(nc.scalar.copy, 1, w0_g[:, HID * 4 :])
+        for i in range(1, LAST):
+            widen_s(i + 1, 1, 0)
+            widen_s(i + 1, 1, 1)
+            widen_v(i, 0, 0)
+            if i == 1:
+                interleave(1, 1)
+                quantize_w(w0_g, w0_c, w0_s)
+            quantize_x(i - 1, 1)
+            layer1(i - 1, 0)
+            layer1(i - 1, HALF)
+            widen_v(i, 0, 1)
+            if i == 1:
+                weights_out(nc.vector.tensor_copy, 2, w1_g[:])
+            if i >= 2:
+                quantize_h(i - 2)
+                layer2(i - 2)
+            hidden("S", i - 1, 0)
+            hidden("S", i - 1, HALF)
+            if i > 1:
+                interleave(i, 1)
+            quantize_x(i, 0)
+            if i == 1:
+                quantize_w(w1_g, w1_c, w1_s)
+            if i >= 2:
+                finish("V" if i < 6 else "S", i - 2)
+        quantize_x(LAST - 1, 1)
+        layer1(LAST - 1, 0)
+        layer1(LAST - 1, HALF)
+        widen_s(LAST, 0, 0, 0, HALF)
+        widen_s(LAST, 0, 1, 0, HALF)
+        interleave(LAST, 1)
+        hidden("S", LAST - 1, 0)
+        hidden("S", LAST - 1, HALF)
+        quantize_h(LAST - 2)
+        layer2(LAST - 2)
+        quantize_x(LAST, 1)
+        interleave(LAST, 0, 0, HALF)
+        finish("V", LAST - 2)
+        widen_s(LAST, 0, 0, HALF, HALF)
+        widen_s(LAST, 0, 1, HALF, HALF)
+        quantize_x(LAST, 0, 0, HALF)
+        layer1(LAST, 0)
+        quantize_h(LAST - 1)
+        layer2(LAST - 1)
+        interleave(LAST, 0, HALF, HALF)
+        hidden("S", LAST, 0)
+        finish("V", LAST - 1)
+        quantize_x(LAST, 0, HALF, HALF)
+        layer1(LAST, HALF, HALF // 2)
+        layer1(LAST, HALF + HALF // 2, HALF // 2)
+        quantize_h(LAST, 0, R // 2)
+        layer2(LAST, 0, R // 2)
+        hidden("S", LAST, HALF, HALF // 2)
+        hidden("V", LAST, HALF + HALF // 2, HALF // 2)
+        finish("S", LAST, 0, R // 2)
+        quantize_h(LAST, R // 2, R // 2)
+        layer2(LAST, R // 2, R // 2)
+        finish("V", LAST, R // 2, R // 2)

@@ -45,11 +45,11 @@ def tile_cnn_pa_t_kernel(tc, x_bytes, x_scale, w0, w1, out):
             x_sb.append(x_t)
         w0_sb = keep.tile([P, 2 * 2 * CIN], BF16, name="w0_sb", align_bytes=64)
         w1_sb = keep.tile([P, 2 * 2 * HID], BF16, name="w1_sb", align_bytes=64)
-        for g, c in ((1, 0), (0, 0), (1, 1), (0, 1)):
+        for g, c in ((0, 1), (0, 0), (1, 1), (1, 0)):
             nc.sync.dma_start(out=x_sb[0][:, g, c * D : (c + 1) * D], in_=xv[0][:, g, c * D : (c + 1) * D])
-        nc.sync.dma_start(out=x_sb[1][:, 1, :], in_=xv[1][:, 1, :])
-        nc.sync.dma_start(out=w0_sb[:], in_=w0.rearrange("(m t) c k -> m (t c k)", t=2))
         nc.sync.dma_start(out=x_sb[1][:, 0, :], in_=xv[1][:, 0, :])
+        nc.sync.dma_start(out=w0_sb[:], in_=w0.rearrange("(m t) c k -> m (t c k)", t=2))
+        nc.sync.dma_start(out=x_sb[1][:, 1, :], in_=xv[1][:, 1, :])
         nc.sync.dma_start(out=w1_sb[:], in_=w1.rearrange("(m t) c k -> m (t c k)", t=2))
         for b in range(2, BS):
             nc.sync.dma_start(out=x_sb[b][:], in_=xv[b])
@@ -92,24 +92,13 @@ def tile_cnn_pa_t_kernel(tc, x_bytes, x_scale, w0, w1, out):
         def x_values(b, g, c, lo=0, n=Q):
             return x_sb[b][:, g, c * D + 2 * lo : c * D + 2 * (lo + n)].bitcast(FP8)
 
-        def widen_v(b, g, c):
-            grp = new(("grp", b, g), work, [P, Q * 4], BF16, "grp%d" % g)
-            nc.vector.tensor_scalar(
-                out=grp[:].rearrange("p (q c k) -> p q c k", c=2, k=2)[:, :, c, :],
-                in0=x_values(b, g, c).rearrange("p (q k) -> p q k", k=2),
-                scalar1=sc[:, g, c : c + 1],
-                scalar2=None,
-                op0=ALU.mult,
-            )
-
-        def widen_s(b, g, c, lo=0, n=Q):
+        def widen(engine, b, g, c):
             tmp = new(("tmp", b, g), work, [P, 2, D], BF16, "tmp%d" % g)
-            nc.scalar.activation(
-                out=tmp[:, c, 2 * lo : 2 * (lo + n)],
-                in_=x_values(b, g, c, lo, n),
-                func=ACT.Copy,
-                scale=sc[:, g, c : c + 1],
-            )
+            factor = sc[:, g, c : c + 1]
+            if engine == "S":
+                nc.scalar.activation(out=tmp[:, c, :], in_=x_values(b, g, c), func=ACT.Copy, scale=factor)
+            else:
+                nc.vector.tensor_scalar(out=tmp[:, c, :], in0=x_values(b, g, c), scalar1=factor, scalar2=None, op0=ALU.mult)
 
         def interleave(b, g, lo=0, n=Q):
             grp = new(("grp", b, g), work, [P, Q * 4], BF16, "grp%d" % g)
@@ -191,73 +180,81 @@ def tile_cnn_pa_t_kernel(tc, x_bytes, x_scale, w0, w1, out):
             nc.vector.quantize_mx(out=codes[:].bitcast(FP8X4), scales=scales[:], in_=src[:])
 
         LAST = BS - 1
-        for c in range(2):
-            widen_s(0, 1, c)
-            widen_v(0, 0, c)
-        quantize_x(0, 0)
-        for c in range(2):
-            widen_s(1, 1, c)
-        interleave(0, 1)
+        widen("S", 0, 0, 1)
+        widen("V", 0, 0, 0)
+        widen("S", 0, 1, 1)
+        widen("V", 0, 1, 0)
+        widen("S", 1, 0, 1)
         transpose_weights(w0_sb, 512, 0, 0)
         transpose_weights(w0_sb, 512, 256, 1)
         transpose_weights(w1_sb, 256, 0, 2)
         weights_out(nc.scalar.copy, 0, w0_g[:, 0 : HID * 4])
         weights_out(nc.scalar.copy, 1, w0_g[:, HID * 4 :])
-        for i in range(1, LAST):
-            widen_s(i + 1, 1, 0)
-            widen_s(i + 1, 1, 1)
-            widen_v(i, 0, 0)
-            if i == 1:
-                interleave(1, 1)
-                quantize_w(w0_g, w0_c, w0_s)
+        interleave(0, 0)
+        widen("V", 1, 0, 0)
+        interleave(0, 1)
+        quantize_x(0, 0)
+        widen("S", 1, 1, 1)
+        quantize_x(0, 1)
+        interleave(1, 0)
+        quantize_w(w0_g, w0_c, w0_s)
+        widen("V", 1, 1, 0)
+        layer1(0, 0)
+        layer1(0, HALF)
+        quantize_x(1, 0)
+        weights_out(nc.vector.tensor_copy, 2, w1_g[:])
+        interleave(1, 1)
+        widen("S", 2, 0, 1)
+        widen("S", 2, 1, 1)
+        hidden("S", 0, 0)
+        hidden("S", 0, HALF)
+        for i in range(2, LAST):
+            widen("S", i + 1, 0, 1)
+            widen("S", i + 1, 1, 1)
+            widen("V", i, 0, 0)
             quantize_x(i - 1, 1)
             layer1(i - 1, 0)
             layer1(i - 1, HALF)
-            widen_v(i, 0, 1)
-            if i == 1:
-                weights_out(nc.vector.tensor_copy, 2, w1_g[:])
-            if i >= 2:
-                quantize_h(i - 2)
-                layer2(i - 2)
+            interleave(i, 0)
+            if i == 2:
+                quantize_w(w1_g, w1_c, w1_s)
+            widen("V", i, 1, 0)
+            quantize_h(i - 2)
+            layer2(i - 2)
+            quantize_x(i, 0)
             hidden("S", i - 1, 0)
             hidden("S", i - 1, HALF)
-            if i > 1:
-                interleave(i, 1)
-            quantize_x(i, 0)
-            if i == 1:
-                quantize_w(w1_g, w1_c, w1_s)
-            if i >= 2:
-                finish("V" if i < 6 else "S", i - 2)
+            interleave(i, 1)
+            finish("V" if i in () else "S", i - 2)
+        widen("S", LAST, 1, 0)
+        widen("V", LAST, 0, 0)
         quantize_x(LAST - 1, 1)
         layer1(LAST - 1, 0)
         layer1(LAST - 1, HALF)
-        widen_s(LAST, 0, 0, 0, HALF)
-        widen_s(LAST, 0, 1, 0, HALF)
-        interleave(LAST, 1)
-        hidden("S", LAST - 1, 0)
-        hidden("S", LAST - 1, HALF)
+        interleave(LAST, 0)
         quantize_h(LAST - 2)
         layer2(LAST - 2)
-        quantize_x(LAST, 1)
-        interleave(LAST, 0, 0, HALF)
-        finish("V", LAST - 2)
-        widen_s(LAST, 0, 0, HALF, HALF)
-        widen_s(LAST, 0, 1, HALF, HALF)
-        quantize_x(LAST, 0, 0, HALF)
+        interleave(LAST, 1, 0, HALF)
+        quantize_x(LAST, 0)
+        hidden("S", LAST - 1, 0)
+        quantize_x(LAST, 1, 0, HALF)
         layer1(LAST, 0)
-        quantize_h(LAST - 1)
-        layer2(LAST - 1)
-        interleave(LAST, 0, HALF, HALF)
-        hidden("S", LAST, 0)
-        finish("V", LAST - 1)
-        quantize_x(LAST, 0, HALF, HALF)
+        interleave(LAST, 1, HALF, HALF)
+        hidden("S", LAST - 1, HALF)
+        finish("S", LAST - 2)
+        quantize_h(LAST - 1, 0, R // 2)
+        quantize_x(LAST, 1, HALF, HALF)
         layer1(LAST, HALF, HALF // 2)
         layer1(LAST, HALF + HALF // 2, HALF // 2)
+        quantize_h(LAST - 1, R // 2, R // 2)
+        layer2(LAST - 1)
+        hidden("S", LAST, 0)
+        hidden("V", LAST, HALF, HALF // 2)
         quantize_h(LAST, 0, R // 2)
         layer2(LAST, 0, R // 2)
-        hidden("S", LAST, HALF, HALF // 2)
-        hidden("V", LAST, HALF + HALF // 2, HALF // 2)
-        finish("S", LAST, 0, R // 2)
+        hidden("S", LAST, HALF + HALF // 2, HALF // 2)
+        finish("V", LAST - 1)
         quantize_h(LAST, R // 2, R // 2)
         layer2(LAST, R // 2, R // 2)
+        finish("S", LAST, 0, R // 2)
         finish("V", LAST, R // 2, R // 2)

@@ -32,12 +32,17 @@ def tile_cnn_pa_t_kernel(tc, x_bytes, x_scale, w0, w1, out):
     with ExitStack() as ctx:
         keep = ctx.enter_context(tc.tile_pool(name="keep", bufs=1))
         xin = ctx.enter_context(tc.tile_pool(name="xin", bufs=8))
+        outp = ctx.enter_context(tc.tile_pool(name="outp", bufs=4))
         work = ctx.enter_context(tc.tile_pool(name="work", bufs=3))
         psum = ctx.enter_context(tc.psum_pool(name="psum", bufs=4))
         ctx.enter_context(tc.manual_schedule())
 
-        sc = keep.tile([P, G, 2], F32, name="sc")
-        nc.scalar.dma_start(out=sc[:], in_=x_scale.rearrange("o (g p c) x -> p (o g) (c x)", g=G, p=P, c=2))
+        scale_rows = x_scale.rearrange("o (g p c) x -> g p (o c x)", g=G, p=P, c=2)
+        sc = []
+        for g in range(G):
+            sc_g = keep.tile([P, 2], F32, name="sc_%d" % g)
+            nc.scalar.dma_start(out=sc_g[:], in_=scale_rows[g])
+            sc.append(sc_g)
         xv = x_bytes.rearrange("b (g p c) d -> b p g (c d)", g=G, p=P, c=2)
         x_sb = []
         for b in range(BS):
@@ -93,42 +98,42 @@ def tile_cnn_pa_t_kernel(tc, x_bytes, x_scale, w0, w1, out):
             return x_sb[b][:, g, c * D + 2 * lo : c * D + 2 * (lo + n)].bitcast(FP8)
 
         def widen(engine, b, g, c):
-            tmp = new(("tmp", b, g), work, [P, 2, D], BF16, "tmp%d" % g)
-            factor = sc[:, g, c : c + 1]
+            tmp = new(("tmp", b), work, [P, G, 2, D], BF16, "tmp")
+            factor = sc[g][:, c : c + 1]
             if engine == "S":
-                nc.scalar.activation(out=tmp[:, c, :], in_=x_values(b, g, c), func=ACT.Copy, scale=factor)
+                nc.scalar.activation(out=tmp[:, g, c, :], in_=x_values(b, g, c), func=ACT.Copy, scale=factor)
             else:
-                nc.vector.tensor_scalar(out=tmp[:, c, :], in0=x_values(b, g, c), scalar1=factor, scalar2=None, op0=ALU.mult)
+                nc.vector.tensor_scalar(out=tmp[:, g, c, :], in0=x_values(b, g, c), scalar1=factor, scalar2=None, op0=ALU.mult)
 
-        def interleave(b, g, lo=0, n=Q):
-            grp = new(("grp", b, g), work, [P, Q * 4], BF16, "grp%d" % g)
-            words = state["tmp", b, g][:].rearrange("p c d -> p (c d)").bitcast(F32)
+        def interleave(b, g0=0, g1=G, lo=0, n=Q):
+            grp = new(("grp", b), work, [P, G * Q * 4], BF16, "grp")
+            words = state["tmp", b][:].rearrange("p g c d -> p (g c d)").bitcast(F32)
             nc.vector.tensor_copy(
-                out=grp[:, 4 * lo : 4 * (lo + n)].bitcast(F32).rearrange("p (q c) -> p q c", c=2),
-                in_=words.rearrange("p (c q) -> p q c", c=2)[:, lo : lo + n, :],
+                out=grp[:].bitcast(F32).rearrange("p (g q c) -> p g q c", g=G, c=2)[:, g0:g1, lo : lo + n, :],
+                in_=words.rearrange("p (g c q) -> p g q c", g=G, c=2)[:, g0:g1, lo : lo + n, :],
             )
 
-        def quantize_x(b, g, lo=0, n=Q):
-            codes = new(("xc", b, g), work, [P, Q], U32, "xc%d" % g)
-            scales = new(("xs", b, g), work, [P, Q], U8, "xs%d" % g)
+        def quantize_x(b, lo=0, n=G * Q):
+            codes = new(("xc", b), work, [P, G * Q], U32, "xc")
+            scales = new(("xs", b), work, [P, G * Q], U8, "xs")
             nc.vector.quantize_mx(
                 out=codes[:, lo : lo + n].bitcast(FP8X4),
                 scales=scales[:, lo : lo + n],
-                in_=state["grp", b, g][:, 4 * lo : 4 * (lo + n)],
+                in_=state["grp", b][:, 4 * lo : 4 * (lo + n)],
             )
 
         def layer1(b, lo, n=HALF):
             bank = psum.tile([P, 2, n], F32, name="bank1", tag="bank1")
-            cols = slice(lo, lo + n)
             for t in range(2):
                 for g in range(G):
+                    cols = slice(g * Q + lo, g * Q + lo + n)
                     wcols = slice(g * HID + t * P, g * HID + (t + 1) * P)
                     nc.tensor.matmul_mx(
                         out=bank[:, t, :],
                         lhsT=w0_c[:, wcols].bitcast(FP8X4),
                         lhsT_scale=w0_s[:, wcols],
-                        rhs=state["xc", b, g][:, cols].bitcast(FP8X4),
-                        rhs_scale=state["xs", b, g][:, cols],
+                        rhs=state["xc", b][:, cols].bitcast(FP8X4),
+                        rhs_scale=state["xs", b][:, cols],
                         start=(g == 0),
                         stop=(g == G - 1),
                     )
@@ -168,7 +173,7 @@ def tile_cnn_pa_t_kernel(tc, x_bytes, x_scale, w0, w1, out):
             state["bank2", b, lo] = bank
 
         def finish(engine, b, lo=0, n=R):
-            o_sb = work.tile([P, 2, n], F32, name="o_sb", tag="o_sb")
+            o_sb = outp.tile([P, 2, n], F32, name="o_sb", tag="o_sb")
             bank = state["bank2", b, lo]
             if engine == "S":
                 nc.scalar.activation(out=o_sb[:], in_=bank[:], func=ACT.Relu, scale=SCALE1)
@@ -190,63 +195,60 @@ def tile_cnn_pa_t_kernel(tc, x_bytes, x_scale, w0, w1, out):
         transpose_weights(w1_sb, 256, 0, 2)
         weights_out(nc.scalar.copy, 0, w0_g[:, 0 : HID * 4])
         weights_out(nc.scalar.copy, 1, w0_g[:, HID * 4 :])
-        interleave(0, 0)
+        interleave(0, 0, 1)
         widen("V", 1, 0, 0)
-        interleave(0, 1)
-        quantize_x(0, 0)
+        interleave(0, 1, 2)
+        quantize_x(0, 0, Q)
         widen("S", 1, 1, 1)
-        quantize_x(0, 1)
-        interleave(1, 0)
-        quantize_w(w0_g, w0_c, w0_s)
+        quantize_x(0, Q, Q)
         widen("V", 1, 1, 0)
+        quantize_w(w0_g, w0_c, w0_s)
         layer1(0, 0)
         layer1(0, HALF)
-        quantize_x(1, 0)
         weights_out(nc.vector.tensor_copy, 2, w1_g[:])
-        interleave(1, 1)
+        interleave(1)
         widen("S", 2, 0, 1)
         widen("S", 2, 1, 1)
-        hidden("S", 0, 0)
-        hidden("S", 0, HALF)
+        quantize_w(w1_g, w1_c, w1_s)
         for i in range(2, LAST):
+            hidden("S", i - 2, 0)
+            hidden("S", i - 2, HALF)
             widen("S", i + 1, 0, 1)
             widen("S", i + 1, 1, 1)
+            if i + 1 == LAST:
+                widen("S", LAST, 1, 0)
             widen("V", i, 0, 0)
-            quantize_x(i - 1, 1)
+            widen("V", i, 1, 0)
+            quantize_x(i - 1)
             layer1(i - 1, 0)
             layer1(i - 1, HALF)
-            interleave(i, 0)
-            if i == 2:
-                quantize_w(w1_g, w1_c, w1_s)
-            widen("V", i, 1, 0)
             quantize_h(i - 2)
             layer2(i - 2)
-            quantize_x(i, 0)
-            hidden("S", i - 1, 0)
-            hidden("S", i - 1, HALF)
-            interleave(i, 1)
-            finish("V" if i in () else "S", i - 2)
-        widen("S", LAST, 1, 0)
+            interleave(i)
+            if i >= 3:
+                finish("S", i - 3)
+        hidden("S", LAST - 2, 0)
+        hidden("S", LAST - 2, HALF)
         widen("V", LAST, 0, 0)
-        quantize_x(LAST - 1, 1)
+        quantize_x(LAST - 1)
         layer1(LAST - 1, 0)
         layer1(LAST - 1, HALF)
-        interleave(LAST, 0)
+        finish("S", LAST - 3)
+        interleave(LAST, 0, G, 0, HALF)
+        hidden("S", LAST - 1, 0)
+        hidden("S", LAST - 1, HALF)
+        interleave(LAST, 0, G, HALF, HALF)
         quantize_h(LAST - 2)
         layer2(LAST - 2)
-        interleave(LAST, 1, 0, HALF)
-        quantize_x(LAST, 0)
-        hidden("S", LAST - 1, 0)
-        quantize_x(LAST, 1, 0, HALF)
+        quantize_x(LAST, 0, HALF)
+        quantize_x(LAST, Q, HALF)
         layer1(LAST, 0)
-        interleave(LAST, 1, HALF, HALF)
-        hidden("S", LAST - 1, HALF)
-        finish("S", LAST - 2)
-        quantize_h(LAST - 1, 0, R // 2)
-        quantize_x(LAST, 1, HALF, HALF)
+        quantize_x(LAST, HALF, HALF)
+        quantize_x(LAST, Q + HALF, HALF)
         layer1(LAST, HALF, HALF // 2)
         layer1(LAST, HALF + HALF // 2, HALF // 2)
-        quantize_h(LAST - 1, R // 2, R // 2)
+        finish("S", LAST - 2)
+        quantize_h(LAST - 1)
         layer2(LAST - 1)
         hidden("S", LAST, 0)
         hidden("V", LAST, HALF, HALF // 2)

import math
from contextlib import ExitStack

import concourse.mybir as mybir
from concourse.masks import make_identity

BS, CIN, HID, D, OUT_DIM = 8, 512, 256, 1024, 256
P = 128
Q = D // 2
R = Q // 2
G = 2
HALF = Q // 2

FLOPS = 2 * BS * Q * HID * (2 * CIN) + 2 * BS * R * OUT_DIM * (2 * HID)

F32 = mybir.dt.float32
BF16 = mybir.dt.bfloat16
U32 = mybir.dt.uint32
U8 = mybir.dt.uint8
FP8 = mybir.dt.float8_e4m3fn
FP8X4 = mybir.dt.float8_e4m3fn_x4
ACT = mybir.ActivationFunctionType
ALU = mybir.AluOpType

SCALE0 = 1.0 / math.sqrt(CIN)
SCALE1 = 1.0 / math.sqrt(HID)


def tile_cnn_pa_t_kernel(tc, x_bytes, x_scale, w0, w1, out):
    nc = tc.nc

    with ExitStack() as ctx:
        keep = ctx.enter_context(tc.tile_pool(name="keep", bufs=1))
        xin = ctx.enter_context(tc.tile_pool(name="xin", bufs=8))
        outp = ctx.enter_context(tc.tile_pool(name="outp", bufs=4))
        work = ctx.enter_context(tc.tile_pool(name="work", bufs=3))
        psum = ctx.enter_context(tc.psum_pool(name="psum", bufs=4))
        ctx.enter_context(tc.manual_schedule())

        scale_rows = x_scale.rearrange("o (g p c) x -> g p (o c x)", g=G, p=P, c=2)
        sc = []
        for g in range(G):
            sc_g = keep.tile([P, 2], F32, name="sc_%d" % g)
            nc.scalar.dma_start(out=sc_g[:], in_=scale_rows[g])
            sc.append(sc_g)
        xv = x_bytes.rearrange("b (g p c) d -> b p g (c d)", g=G, p=P, c=2)
        x_sb = []
        for b in range(BS):
            x_t = xin.tile([P, G, 2 * D], U8, name="x_t", align_bytes=64)
            x_sb.append(x_t)
        w0_sb = keep.tile([P, 2 * 2 * CIN], BF16, name="w0_sb", align_bytes=64)
        w1_sb = keep.tile([P, 2 * 2 * HID], BF16, name="w1_sb", align_bytes=64)
        for g, c in ((0, 1), (0, 0), (1, 1), (1, 0)):
            nc.sync.dma_start(out=x_sb[0][:, g, c * D : (c + 1) * D], in_=xv[0][:, g, c * D : (c + 1) * D])
        nc.sync.dma_start(out=x_sb[1][:, 0, :], in_=xv[1][:, 0, :])
        nc.sync.dma_start(out=w0_sb[:], in_=w0.rearrange("(m t) c k -> m (t c k)", t=2))
        nc.sync.dma_start(out=x_sb[1][:, 1, :], in_=xv[1][:, 1, :])
        nc.sync.dma_start(out=w1_sb[:], in_=w1.rearrange("(m t) c k -> m (t c k)", t=2))
        for b in range(2, BS):
            nc.sync.dma_start(out=x_sb[b][:], in_=xv[b])

        warm = keep.tile([P, 1], F32, name="warm")
        nc.vector.memset(warm[:], 0.0)
        nc.scalar.activation(out=warm[:], in_=warm[:], func=ACT.Relu)
        ident = keep.tile([P, P], F32, name="ident")
        make_identity(nc, ident[:])

        w0_c = keep.tile([P, G * HID], U32, name="w0_c", align_bytes=64)
        w0_s = keep.tile([P, G * HID], U8, name="w0_s", align_bytes=64)
        w0_g = keep.tile([P, G * HID * 4], BF16, name="w0_g", align_bytes=64)
        w1_c = keep.tile([P, OUT_DIM], U32, name="w1_c", align_bytes=64)
        w1_s = keep.tile([P, OUT_DIM], U8, name="w1_s", align_bytes=64)
        w1_g = keep.tile([P, OUT_DIM * 4], BF16, name="w1_g", align_bytes=64)

        state = {}

        def new(key, pool, shape, dtype, name):
            if key not in state:
                state[key] = pool.tile(shape, dtype, name=name, align_bytes=64)
            return state[key]

        def transpose_weights(w_sb, row, first, key):
            words = w_sb[:].bitcast(F32)
            bank = psum.tile([P, 2, 2, P], F32, name="bank2", tag="bank2")
            for t in range(2):
                for u in range(2):
                    lo = row * t + first
                    nc.tensor.transpose(bank[:, t, u, :], words[:, lo + u : lo + 256 : 2], ident[:])
            state[key] = bank

        def weights_out(engine_copy, key, dst):
            engine_copy(
                out=dst.bitcast(F32).rearrange("p (t m u) -> p t m u", t=2, u=2),
                in_=state[key][:].rearrange("p t u m -> p t m u"),
            )

        def x_values(b, g, c, lo=0, n=Q):
            return x_sb[b][:, g, c * D + 2 * lo : c * D + 2 * (lo + n)].bitcast(FP8)

        def widen(engine, b, g, c):
            tmp = new(("tmp", b), work, [P, G, 2, D], BF16, "tmp")
            factor = sc[g][:, c : c + 1]
            if engine == "S":
                nc.scalar.activation(out=tmp[:, g, c, :], in_=x_values(b, g, c), func=ACT.Copy, scale=factor)
            else:
                nc.vector.tensor_scalar(out=tmp[:, g, c, :], in0=x_values(b, g, c), scalar1=factor, scalar2=None, op0=ALU.mult)

        def interleave(b, g0=0, g1=G, lo=0, n=Q):
            grp = new(("grp", b), work, [P, G * Q * 4], BF16, "grp")
            words = state["tmp", b][:].rearrange("p g c d -> p (g c d)").bitcast(F32)
            nc.vector.tensor_copy(
                out=grp[:].bitcast(F32).rearrange("p (g q c) -> p g q c", g=G, c=2)[:, g0:g1, lo : lo + n, :],
                in_=words.rearrange("p (g c q) -> p g q c", g=G, c=2)[:, g0:g1, lo : lo + n, :],
            )

        def quantize_x(b, lo=0, n=G * Q):
            codes = new(("xc", b), work, [P, G * Q], U32, "xc")
            scales = new(("xs", b), work, [P, G * Q], U8, "xs")
            nc.vector.quantize_mx(
                out=codes[:, lo : lo + n].bitcast(FP8X4),
                scales=scales[:, lo : lo + n],
                in_=state["grp", b][:, 4 * lo : 4 * (lo + n)],
            )

        def layer1(b, lo, n=HALF):
            bank = psum.tile([P, 2, n], F32, name="bank1", tag="bank1")
            for t in range(2):
                for g in range(G):
                    cols = slice(g * Q + lo, g * Q + lo + n)
                    wcols = slice(g * HID + t * P, g * HID + (t + 1) * P)
                    nc.tensor.matmul_mx(
                        out=bank[:, t, :],
                        lhsT=w0_c[:, wcols].bitcast(FP8X4),
                        lhsT_scale=w0_s[:, wcols],
                        rhs=state["xc", b][:, cols].bitcast(FP8X4),
                        rhs_scale=state["xs", b][:, cols],
                        start=(g == 0),
                        stop=(g == G - 1),
                    )
            state["bank1", b, lo] = bank

        def hidden(engine, b, lo, n=HALF):
            h = new(("h", b), work, [P, R * 4], BF16, "hgrp")
            dst = h[:, 2 * lo : 2 * (lo + n)].rearrange("p (r c k) -> p r c k", c=2, k=2)
            z = state["bank1", b, lo][:].rearrange("p c (r k) -> p r c k", k=2)
            if engine == "S":
                nc.scalar.activation(out=dst, in_=z, func=ACT.Relu, scale=SCALE0)
            else:
                nc.vector.tensor_scalar(out=dst, in0=z, scalar1=SCALE0, scalar2=0.0, op0=ALU.mult, op1=ALU.max)

        def quantize_h(b, lo=0, n=R):
            codes = new(("hc", b), work, [P, R], U32, "hc")
            scales = new(("hs", b), work, [P, R], U8, "hs")
            nc.vector.quantize_mx(
                out=codes[:, lo : lo + n].bitcast(FP8X4),
                scales=scales[:, lo : lo + n],
                in_=state["h", b][:, 4 * lo : 4 * (lo + n)],
            )

        def layer2(b, lo=0, n=R):
            bank = psum.tile([P, 2, n], F32, name="bank2", tag="bank2")
            for t in range(2):
                wcols = slice(t * P, (t + 1) * P)
                nc.tensor.matmul_mx(
                    out=bank[:, t, :],
                    lhsT=w1_c[:, wcols].bitcast(FP8X4),
                    lhsT_scale=w1_s[:, wcols],
                    rhs=state["hc", b][:, lo : lo + n].bitcast(FP8X4),
                    rhs_scale=state["hs", b][:, lo : lo + n],
                    start=True,
                    stop=True,
                )
            state["bank2", b, lo] = bank

        def finish(engine, b, lo=0, n=R):
            o_sb = outp.tile([P, 2, n], F32, name="o_sb", tag="o_sb")
            bank = state["bank2", b, lo]
            if engine == "S":
                nc.scalar.activation(out=o_sb[:], in_=bank[:], func=ACT.Relu, scale=SCALE1)
            else:
                nc.vector.tensor_scalar(out=o_sb[:], in0=bank[:], scalar1=SCALE1, scalar2=0.0, op0=ALU.mult, op1=ALU.max)
            nc.sync.dma_start(out=out[b].rearrange("(m t) r -> m t r", t=2)[:, :, lo : lo + n], in_=o_sb[:])

        def quantize_w(src, codes, scales):
            nc.vector.quantize_mx(out=codes[:].bitcast(FP8X4), scales=scales[:], in_=src[:])

        LAST = BS - 1
        widen("S", 0, 0, 1)
        widen("V", 0, 0, 0)
        widen("S", 0, 1, 1)
        widen("V", 0, 1, 0)
        widen("S", 1, 0, 1)
        transpose_weights(w0_sb, 512, 0, 0)
        transpose_weights(w0_sb, 512, 256, 1)
        transpose_weights(w1_sb, 256, 0, 2)
        weights_out(nc.scalar.copy, 0, w0_g[:, 0 : HID * 4])
        weights_out(nc.scalar.copy, 1, w0_g[:, HID * 4 :])
        interleave(0, 0, 1)
        widen("V", 1, 0, 0)
        interleave(0, 1, 2)
        quantize_x(0, 0, Q)
        widen("S", 1, 1, 1)
        quantize_x(0, Q, Q)
        widen("V", 1, 1, 0)
        quantize_w(w0_g, w0_c, w0_s)
        layer1(0, 0)
        layer1(0, HALF)
        weights_out(nc.vector.tensor_copy, 2, w1_g[:])
        interleave(1)
        widen("S", 2, 0, 1)
        widen("S", 2, 1, 1)
        quantize_w(w1_g, w1_c, w1_s)
        for i in range(2, LAST):
            hidden("S", i - 2, 0)
            hidden("S", i - 2, HALF)
            widen("S", i + 1, 0, 1)
            widen("S", i + 1, 1, 1)
            if i + 1 == LAST:
                widen("S", LAST, 1, 0)
            widen("V", i, 0, 0)
            widen("V", i, 1, 0)
            quantize_x(i - 1)
            layer1(i - 1, 0)
            layer1(i - 1, HALF)
            quantize_h(i - 2)
            layer2(i - 2)
            interleave(i)
            if i >= 3:
                finish("S", i - 3)
        hidden("S", LAST - 2, 0)
        hidden("S", LAST - 2, HALF)
        widen("V", LAST, 0, 0)
        quantize_x(LAST - 1)
        layer1(LAST - 1, 0)
        layer1(LAST - 1, HALF)
        finish("S", LAST - 3)
        interleave(LAST, 0, G, 0, HALF)
        hidden("S", LAST - 1, 0)
        hidden("S", LAST - 1, HALF)
        interleave(LAST, 0, G, HALF, HALF)
        quantize_h(LAST - 2)
        layer2(LAST - 2)
        quantize_x(LAST, 0, HALF)
        quantize_x(LAST, Q, HALF)
        layer1(LAST, 0)
        quantize_x(LAST, HALF, HALF)
        quantize_x(LAST, Q + HALF, HALF)
        layer1(LAST, HALF, HALF // 2)
        layer1(LAST, HALF + HALF // 2, HALF // 2)
        finish("S", LAST - 2)
        quantize_h(LAST - 1)
        layer2(LAST - 1)
        hidden("S", LAST, 0)
        hidden("V", LAST, HALF, HALF // 2)
        quantize_h(LAST, 0, R // 2)
        layer2(LAST, 0, R // 2)
        hidden("S", LAST, HALF + HALF // 2, HALF // 2)
        finish("V", LAST - 1)
        quantize_h(LAST, R // 2, R // 2)
        layer2(LAST, R // 2, R // 2)
        finish("S", LAST, 0, R // 2)
        finish("V", LAST, R // 2, R // 2)
